import numpy as np
import ml_dtypes


def mxq(x, axis, fmt="e4m3"):
    dtype, down = {"e4m3": (ml_dtypes.float8_e4m3fn, 7), "e5m2": (ml_dtypes.float8_e5m2, 14)}[fmt]
    v = np.moveaxis(np.asarray(x, np.float32).astype(ml_dtypes.bfloat16).astype(np.float64), axis, -1)
    blocks = v.reshape(v.shape[:-1] + (-1, 32))
    amax = np.abs(blocks).max(-1, keepdims=True)
    byte = np.maximum(np.where(amax > 0, np.frexp(amax)[1] - 1 + 127, 0) - down, 1)
    scale = np.exp2(byte - 127.0)
    codes = (blocks / scale).astype(np.float32).astype(dtype).astype(np.float64)
    return np.moveaxis((codes * scale).reshape(v.shape), -1, axis)


WIDE = False


def mx_kscale(k):
    if not WIDE:
        return np.ones(k)
    levels = np.array([10, -10, 5, -5, 0])
    if k % 512:
        return np.exp2(np.random.permutation(np.resize(levels, k // 32))).repeat(32)
    a = np.empty((k // 512, 16))
    for p in range(k // 512):
        a[p, :8] = np.random.permutation(np.resize(levels, 8))
        for g in range(8):
            far = levels[np.abs(levels - a[p, g]) >= 10]
            a[p, g + 8] = far[np.random.randint(len(far))]
    return np.exp2(a.ravel()).repeat(32)


BF16 = ml_dtypes.bfloat16


def bf(x):
    return np.asarray(x, np.float32).astype(BF16)


def f64(x):
    return np.asarray(x).astype(np.float64)


E2M1 = np.array([0.0, 0.5, 1.0, 1.5, 2.0, 3.0, 4.0, 6.0, -0.0, -0.5, -1.0, -1.5, -2.0, -3.0, -4.0, -6.0])


def pack_weight(w, fmt):
    k, n = w.shape
    w = f64(bf(w)).reshape(k // 32, 32, n)
    amax = np.abs(w).max(1)
    if fmt == "e4m3":
        byte = np.frexp(amax)[1] - 1 + 127 - 7
    else:
        mant, ex = np.frexp(amax / 6.0)
        byte = np.where(mant > 0.5, ex, ex - 1) + 127
    byte = np.clip(np.where(amax > 0, byte, 1), 1, 254)
    scaled = (w * np.exp2(127.0 - byte)[:, None, :]).reshape(k, n).astype(np.float32)
    by_word = np.ascontiguousarray(scaled.reshape(k // 512, 128, 4, n).transpose(0, 1, 3, 2))
    if fmt == "e4m3":
        words = by_word.astype(ml_dtypes.float8_e4m3fn).view(np.uint8)
    else:
        c = by_word.astype(ml_dtypes.float4_e2m1fn).view(np.uint8) & 0xF
        words = c[..., 0::2] | (c[..., 1::2] << 4)
    return np.ascontiguousarray(words), np.ascontiguousarray(byte.astype(np.uint8).reshape(k // 512, 16, n))


def unpack_weight(words, scales, fmt):
    g, p, n, _ = words.shape
    if fmt == "e4m3":
        vals = np.ascontiguousarray(words).view(ml_dtypes.float8_e4m3fn).astype(np.float64)
    else:
        nib = np.empty((g, p, n, 4), np.uint8)
        nib[..., 0::2] = words & 0xF
        nib[..., 1::2] = words >> 4
        vals = E2M1[nib]
    vals = vals * np.repeat(np.exp2(scales.astype(np.float64) - 127.0), 8, axis=1)[..., None]
    return vals.transpose(0, 1, 3, 2).reshape(g * 512, n)


E, D, H, C = 128, 2048, 4096, 128


def silu(v):
    return v / (1.0 + np.exp(-v))


def draw0():
    s = mx_kscale(D)
    t = mx_kscale(H)
    node_embed = bf(np.random.standard_normal((E, D)) * s)
    x_edge_c = bf(np.random.standard_normal((E, H)) * t)
    ori = bf(np.random.standard_normal((E, D)) * s)
    W1_words, W1_scales = pack_weight(np.random.standard_normal((D, H)) * 1.0 / np.sqrt(D) / s[:, None], "e4m3")
    b1 = bf(np.random.standard_normal(H) * 0.3)
    W2_words, W2_scales = pack_weight(np.random.standard_normal((H, D)) * 1.5 / np.sqrt(H) / t[:, None], "e4m3")
    b2 = bf(np.random.standard_normal(D) * 0.3)
    return {
        "node_embed": node_embed,
        "x_edge_c": x_edge_c,
        "ori": ori,
        "W1_words": W1_words,
        "W1_scales": W1_scales,
        "b1": b1,
        "W2_words": W2_words,
        "W2_scales": W2_scales,
        "b2": b2,
        "edge_num": E,
    }


def core(node_embed, x_edge_c, ori, W1_words, W1_scales, b1, W2_words, W2_scales, b2, edge_num):
    x = np.concatenate([f64(node_embed), f64(ori)], axis=0)
    h = silu((mxq(x, 1, "e4m3") @ unpack_weight(W1_words, W1_scales, "e4m3")) + f64(b1))
    h = (h.reshape(2, edge_num, H) * f64(x_edge_c).reshape(1, edge_num, H)).reshape(-1, H)
    y = silu((mxq(h, 1, "e4m3") @ unpack_weight(W2_words, W2_scales, "e4m3")) + f64(b2))
    y = y.reshape(2 * edge_num, -1, C)
    return y[:edge_num] + y[edge_num:]


def e4m3fn_bytes(y):
    return np.clip(np.asarray(y, np.float64), -448.0, 448.0).astype(np.float32).astype(ml_dtypes.float8_e4m3fn).view(np.uint8)


def e4m3fn_values(b):
    return np.asarray(b, np.uint8).view(ml_dtypes.float8_e4m3fn).astype(np.float64)


def setup_inputs():
    d = draw0()
    x0 = np.asarray(d['ori']).astype(np.float64)
    s = (np.max(np.abs(x0), axis=(0,), keepdims=True) / 448.0).astype(np.float32)
    out = {}
    for k, v in d.items():
        if k == 'ori':
            out['ori_bytes'] = e4m3fn_bytes(x0 / s.astype(np.float64))
            out['ori_scale'] = s
        else:
            out[k] = v
    return out


def reference(node_embed, x_edge_c, ori_bytes, ori_scale, W1_words, W1_scales, b1, W2_words, W2_scales, b2, edge_num):
    return core(node_embed, x_edge_c, e4m3fn_values(ori_bytes) * ori_scale.astype(np.float64), W1_words, W1_scales, b1, W2_words, W2_scales, b2, edge_num)

@@ -1,0 +1,328 @@
+from contextlib import ExitStack
+
+import concourse.mybir as mybir
+from concourse.masks import make_identity
+
+E, D, H = 128, 2048, 4096
+FLOPS = 2 * (2 * E) * D * H * 2
+
+F32 = mybir.dt.float32
+BF16 = mybir.dt.bfloat16
+I32 = mybir.dt.int32
+U32 = mybir.dt.uint32
+U8 = mybir.dt.uint8
+FP8 = mybir.dt.float8_e4m3fn
+FP8X4 = mybir.dt.float8_e4m3fn_x4
+ADD = mybir.AluOpType.add
+MULT = mybir.AluOpType.mult
+SILU = mybir.ActivationFunctionType.Silu
+
+P = 128
+KP = 512
+NT = 512
+G1 = D // KP
+G2 = H // KP
+C1 = H // NT
+C2 = D // NT
+
+
+def tile_node_interaction_w_w8_kernel(
+    tc, node_embed, x_edge_c, ori_bytes, ori_scale, W1_words, W1_scales, b1, W2_words, W2_scales, b2, edge_num, out
+):
+    nc = tc.nc
+    assert edge_num == E
+    out2d = out.rearrange("e a c -> e (a c)")
+
+    with ExitStack() as ctx:
+        keep = ctx.enter_context(tc.tile_pool(name="keep", bufs=1))
+        work = ctx.enter_context(tc.tile_pool(name="work", bufs=3))
+        psum = ctx.enter_context(tc.psum_pool(name="psum", bufs=1))
+        ctx.enter_context(tc.manual_schedule())
+
+        def bank(i, shape, dtype):
+            return psum.tile(shape, dtype, name="bank%d" % i, tag="bank%d" % i)
+
+        ident = keep.tile([P, P], F32, name="ident")
+        make_identity(nc, ident[:])
+        b1_rows = keep.tile([P, NT], BF16, name="b1_rows")
+        b2_rows = keep.tile([P, NT], BF16, name="b2_rows")
+        s1 = keep.tile([P, H], U8, name="s1", align_bytes=64)
+        s2 = [keep.tile([P, D], U8, name="s2_%d" % i, align_bytes=64) for i in range(2)]
+        nc.vector.memset(b1_rows[:].bitcast(I32), 0)
+        nc.vector.memset(s1[:].bitcast(I32), 0)
+        pick = keep.tile([P, C1], BF16, name="pick")
+        nc.vector.tensor_copy(out=pick[:], in_=ident[:, 0:C1])
+        nc.vector.memset(b2_rows[:].bitcast(I32), 0)
+        for i in range(2):
+            nc.vector.memset(s2[i][:].bitcast(I32), 0)
+
+        node = keep.tile([P, D], BF16, name="node")
+        nc.sync.dma_start(out=node[:], in_=node_embed)
+        nc.sync.dma_start(out=b1_rows[0:C1, :], in_=b1.rearrange("(c n) -> c n", n=NT))
+        ori_u8 = keep.tile([P, D], U8, name="ori_u8")
+        nc.sync.dma_start(out=ori_u8[:], in_=ori_bytes)
+        ori_s = keep.tile([P, G1, 4], F32, name="ori_s")
+        nc.sync.dma_start(out=ori_s[:], in_=ori_scale.rearrange("o (g p t) -> p (o g) t", p=P, t=4))
+        for q in range(4):
+            nc.sync.dma_start(
+                out=s1[32 * q : 32 * q + 16, :].bitcast(I32), in_=W1_scales[:, 4 * q : 4 * q + 4, :].bitcast(I32)
+            )
+
+        def load_words(words, name, g0, g1, n0, n1):
+            t = keep.tile([P, g1 - g0, n1 - n0], U32, name=name, align_bytes=256)
+            src = words[g0:g1].rearrange("g p n t -> p g (n t)")[:, :, 4 * n0 : 4 * n1].bitcast(I32)
+            nc.sync.dma_start(out=t[:].bitcast(I32), in_=src)
+            return {g: t[:, g - g0, :] for g in range(g0, g1)}
+
+        w1 = []
+        gate = []
+        for c in range(C1):
+            cw = {}
+            for g0 in range(0, G1, 2):
+                cw.update(load_words(W1_words, "w1_%d_%d" % (c, g0), g0, g0 + 2, c * NT, (c + 1) * NT))
+            w1.append(cw)
+            if c % 2 == 0:
+                xe = keep.tile([P, 2 * NT], BF16, name="gate%d" % c)
+                nc.sync.dma_start(out=xe[:], in_=x_edge_c[:, c * NT : (c + 2) * NT])
+                gate.extend([xe[:, 0:NT], xe[:, NT : 2 * NT]])
+            if c == 0:
+                nc.sync.dma_start(out=b2_rows[0:C2, :], in_=b2.rearrange("(c n) -> c n", n=NT))
+        for i in range(2):
+            for q in range(4):
+                nc.sync.dma_start(
+                    out=s2[i][32 * q : 32 * q + 16, :].bitcast(I32),
+                    in_=W2_scales[4 * i : 4 * i + 4, 4 * q : 4 * q + 4, :].bitcast(I32),
+                )
+        w2 = []
+        for n in range(C2 - 1):
+            cw = {}
+            for g0 in range(0, G2, 2):
+                cw.update(load_words(W2_words, "w2_%d_%d" % (n, g0), g0, g0 + 2, n * NT, (n + 1) * NT))
+            w2.append(cw)
+        n0 = (C2 - 1) * NT
+        half = NT // 2
+        wide = {}
+        for g0 in (0, 2):
+            wide.update(load_words(W2_words, "w2_last_%d" % g0, g0, g0 + 2, n0, n0 + NT))
+        w2a = {g: wide[g][:, 0:half] for g in wide}
+        w2b = {g: wide[g][:, half:NT] for g in wide}
+        w2a.update(load_words(W2_words, "w2_a", 4, 8, n0, n0 + half))
+        for g0, g1 in ((4, 6), (6, 7), (7, 8)):
+            w2b.update(load_words(W2_words, "w2_b%d" % g0, g0, g1, n0 + half, n0 + NT))
+
+        bias1 = []
+        bias2 = []
+
+        def spread_matmuls(rows, pair, bank_i):
+            ps = bank(bank_i, [P, 2, NT], BF16)
+            for i in range(2):
+                c = 2 * pair + i
+                nc.tensor.matmul(
+                    out=ps[:, i, :], lhsT=pick[:, c : c + 1].to_broadcast([P, P]), rhs=rows[:], start=True, stop=True
+                )
+            return ps
+
+        def copy_bias1(ps, pair):
+            t = keep.tile([P, 2, NT], BF16, name="bias1_%d" % pair)
+            nc.scalar.copy(
+                out=t[:].bitcast(F32).rearrange("p c (u m) -> p c u m", u=2),
+                in_=ps[:].bitcast(F32).rearrange("p c (m u) -> p c u m", u=2),
+            )
+            bias1.extend([t[:, 0, :], t[:, 1, :]])
+
+        def copy_bias2(ps, pair):
+            t = keep.tile([P, 2, NT], BF16, name="bias2_%d" % pair)
+            nc.scalar.copy(out=t[:], in_=ps[:])
+            bias2.extend([t[:, 0, :], t[:, 1, :]])
+
+        xq = {}
+
+        def quantize(src, name, width):
+            codes = keep.tile([P, width], U32, name=name + "_codes", align_bytes=64)
+            scales = keep.tile([P, width], U8, name=name + "_scales", align_bytes=64)
+            nc.vector.quantize_mx(out=codes[:].bitcast(FP8X4), scales=scales[:], in_=src)
+            return codes, scales
+
+        ps_b = spread_matmuls(b1_rows, 0, 6)
+        copy_bias1(ps_b, 0)
+
+        node_words = node[:].bitcast(F32)
+        node_t = []
+        for pair in range(2):
+            ps = bank(4 + pair, [P, 2, 2, P], F32)
+            for i in range(2):
+                g = 2 * pair + i
+                for u in range(2):
+                    nc.tensor.transpose(ps[:, i, u, :], node_words[:, 256 * g + u : 256 * (g + 1) : 2], ident[:])
+            node_t.append(ps)
+        ori_wide = []
+        for g in range(G1):
+            t = keep.tile([P, KP], BF16, name="ori_wide%d" % g)
+            nc.vector.tensor_copy(
+                out=t[:].rearrange("p (u m e) -> p m u e", u=2, e=2),
+                in_=ori_u8[:, g * KP : (g + 1) * KP].bitcast(FP8).rearrange("p (m u e) -> p m u e", u=2, e=2),
+            )
+            ori_wide.append(t)
+        for g in range(G1):
+            xg = work.tile([P, 4 * P], BF16, name="xg", tag="xg", bufs=4, align_bytes=64)
+            nc.scalar.copy(
+                out=xg[:].bitcast(F32).rearrange("p (r u) -> p r u", u=2),
+                in_=node_t[g // 2][:, g % 2, :, :].rearrange("p u r -> p r u"),
+            )
+            xq[g, 0] = quantize(xg[:], "xq%d_0" % g, P)
+
+        ps_b = spread_matmuls(b1_rows, 1, 7)
+        copy_bias1(ps_b, 1)
+
+        ori_t = []
+        for pair in range(2):
+            ps = bank(2 + pair, [P, 2, 2, P], F32)
+            for i in range(2):
+                words = ori_wide[2 * pair + i][:].bitcast(F32)
+                for u in range(2):
+                    nc.tensor.transpose(ps[:, i, u, :], words[:, P * u : P * (u + 1)], ident[:])
+            ori_t.append(ps)
+        scaled = []
+        for g in range(G1 + 1):
+            if g < G1:
+                xg = work.tile([P, 4 * P], BF16, name="xg", tag="xg", bufs=4, align_bytes=64)
+                src = ori_t[g // 2][:, g % 2, :, :].bitcast(BF16).rearrange("p u (r e) -> p r u e", e=2)
+                fac = ori_s[:, g, :].rearrange("p (u e) -> p u e", u=2).unsqueeze(1).to_broadcast([P, P, 2, 2])
+                nc.vector.tensor_tensor(
+                    out=xg[:].rearrange("p (r u e) -> p r u e", u=2, e=2), in0=src, in1=fac, op=MULT
+                )
+                scaled.append(xg)
+            if g > 0:
+                xq[g - 1, 1] = quantize(scaled[g - 1][:], "xq%d_1" % (g - 1), P)
+
+        def mx(acc, stat, j, words, scale_plane, first, last):
+            codes, scales = stat
+            nc.tensor.matmul_mx(
+                out=acc,
+                lhsT=codes[:, j * P : (j + 1) * P].bitcast(FP8X4),
+                lhsT_scale=scales[:, j * P : (j + 1) * P],
+                rhs=words.bitcast(FP8X4),
+                rhs_scale=scale_plane,
+                start=first,
+                stop=last,
+            )
+
+        h = {}
+        h_t = {}
+        h_grouped = {}
+        hq = {}
+
+        def stage1_matmuls(c):
+            acc = [bank((2 * c + j) % 4, [P, NT], F32) for j in range(2)]
+            for g0 in range(0, G1, 2):
+                for j in range(2):
+                    for g in (g0, g0 + 1):
+                        mx(acc[j][:], xq[g, j], 0, w1[c][g], s1[4 * g : P, c * NT : (c + 1) * NT], g == 0, g == G1 - 1)
+            return acc
+
+        def bias_silu(acc, bias, permute):
+            width = acc.shape[1]
+            pre = work.tile([P, width], F32, name="pre", tag="pre")
+            if permute:
+                nc.vector.tensor_tensor(
+                    out=pre[:].rearrange("p (u m e) -> p u m e", u=2, e=2),
+                    in0=acc.rearrange("p (m u e) -> p u m e", u=2, e=2),
+                    in1=bias.rearrange("p (u m e) -> p u m e", u=2, e=2),
+                    op=ADD,
+                )
+            else:
+                nc.vector.tensor_tensor(out=pre[:], in0=acc, in1=bias, op=ADD)
+            act = work.tile([P, width], F32, name="act", tag="act", bufs=4)
+            nc.scalar.activation(out=act[:], in_=pre[:], func=SILU)
+            return act
+
+        def apply_gate(c, j, act):
+            t = work.tile([P, NT], BF16, name="h", tag="h", bufs=8)
+            nc.vector.tensor_tensor(
+                out=t[:].rearrange("p (u m e) -> p u m e", u=2, e=2),
+                in0=act[:].rearrange("p (u m e) -> p u m e", u=2, e=2),
+                in1=gate[c].rearrange("p (m u e) -> p u m e", u=2, e=2),
+                op=MULT,
+            )
+            h[c, j] = t
+
+        def transpose_h(c):
+            ps = bank(4 + c % 2, [P, 2, 2, P], F32)
+            for j in range(2):
+                words = h[c, j][:].bitcast(F32)
+                for u in range(2):
+                    nc.tensor.transpose(ps[:, j, u, :], words[:, P * u : P * (u + 1)], ident[:])
+            h_t[c] = ps
+
+        def copy_h(c, on_vector):
+            t = work.tile([P, 2 * 4 * P], BF16, name="hg", tag="hg", align_bytes=64)
+            dst = t[:].bitcast(F32).rearrange("p (j r u) -> p j r u", j=2, u=2)
+            src = h_t[c][:].rearrange("p j u r -> p j r u")
+            if on_vector:
+                nc.vector.tensor_copy(out=dst, in_=src)
+            else:
+                nc.scalar.copy(out=dst, in_=src)
+            h_grouped[c] = t
+
+        def quantize_h(c):
+            hq[c] = quantize(h_grouped[c][:], "hq%d" % c, 2 * P)
+
+        for c in range(C1):
+            acc = stage1_matmuls(c)
+            spread = []
+            if c == 0:
+                spread = [spread_matmuls(b1_rows, 2, 6), spread_matmuls(b1_rows, 3, 7)]
+            if c == 1:
+                spread = [spread_matmuls(b2_rows, 0, 6), spread_matmuls(b2_rows, 1, 7)]
+            if c >= 3 and c % 2 == 1:
+                transpose_h(c - 3)
+                transpose_h(c - 2)
+            acts = [bias_silu(acc[j][:], bias1[c], True) for j in range(2)]
+            for i, ps in enumerate(spread):
+                if c == 0:
+                    copy_bias1(ps, 2 + i)
+                else:
+                    copy_bias2(ps, i)
+            if c >= 4:
+                quantize_h(c - 4)
+            if c >= 3 and c % 2 == 1:
+                copy_h(c - 3, False)
+                copy_h(c - 2, False)
+            for j in range(2):
+                apply_gate(c, j, acts[j])
+        quantize_h(4)
+        quantize_h(5)
+
+        def stage2_pass(acc, g, words, n0, n1):
+            for j in range(2):
+                mx(acc[j][:], hq[g], j, words, s2[g // 4][4 * (g % 4) : P, n0:n1], g == 0, g == G2 - 1)
+
+        def finish(acc, bias, n0, n1, name):
+            acts = [bias_silu(acc[j][:], bias, False) for j in range(2)]
+            res = keep.tile([P, n1 - n0], F32, name=name)
+            nc.vector.tensor_tensor(out=res[:], in0=acts[0][:], in1=acts[1][:], op=ADD)
+            nc.sync.dma_start(out=out2d[:, n0:n1], in_=res[:])
+
+        for n in range(C2 - 1):
+            acc = [bank((6 + 2 * n + j) % 8, [P, NT], F32) for j in range(2)]
+            for g in range(G2):
+                if n == 0 and g == 4:
+                    transpose_h(6)
+                    transpose_h(7)
+                    copy_h(6, False)
+                    copy_h(7, True)
+                    quantize_h(6)
+                    quantize_h(7)
+                stage2_pass(acc, g, w2[n][g], n * NT, (n + 1) * NT)
+            finish(acc, bias2[n], n * NT, (n + 1) * NT, "res%d" % n)
+        acc_a = [bank(4 + j, [P, half], F32) for j in range(2)]
+        acc_b = [bank(6 + j, [P, half], F32) for j in range(2)]
+        for g in range(4):
+            stage2_pass(acc_a, g, w2a[g], n0, n0 + half)
+            stage2_pass(acc_b, g, w2b[g], n0 + half, n0 + NT)
+        for g in range(4, G2):
+            stage2_pass(acc_a, g, w2a[g], n0, n0 + half)
+        finish(acc_a, bias2[C2 - 1][:, 0:half], n0, n0 + half, "res_a")
+        for g in range(4, G2):
+            stage2_pass(acc_b, g, w2b[g], n0 + half, n0 + NT)
+        finish(acc_b, bias2[C2 - 1][:, half:NT], n0 + half, n0 + NT, "res_b")

@@ -46,27 +46,27 @@ def tile_node_interaction_w_w8_kernel(
         make_identity(nc, ident[:])
         b1_rows = keep.tile([P, NT], BF16, name="b1_rows")
         b2_rows = keep.tile([P, NT], BF16, name="b2_rows")
-        s1 = keep.tile([P, H], U8, name="s1", align_bytes=64)
+        s1 = [keep.tile([P, 2 * NT], U8, name="s1_%d" % i, align_bytes=64) for i in range(C1 // 2)]
         s2 = [keep.tile([P, D], U8, name="s2_%d" % i, align_bytes=64) for i in range(2)]
-        nc.vector.memset(b1_rows[:].bitcast(I32), 0)
-        nc.vector.memset(s1[:].bitcast(I32), 0)
+        for t in [b1_rows] + s1 + [b2_rows] + s2:
+            nc.vector.memset(t[:].bitcast(I32), 0)
         pick = keep.tile([P, C1], BF16, name="pick")
         nc.vector.tensor_copy(out=pick[:], in_=ident[:, 0:C1])
-        nc.vector.memset(b2_rows[:].bitcast(I32), 0)
-        for i in range(2):
-            nc.vector.memset(s2[i][:].bitcast(I32), 0)
 
-        node = keep.tile([P, D], BF16, name="node")
-        nc.sync.dma_start(out=node[:], in_=node_embed)
-        nc.sync.dma_start(out=b1_rows[0:C1, :], in_=b1.rearrange("(c n) -> c n", n=NT))
+        nc.scalar.dma_start(out=b1_rows[0:C1, :], in_=b1.rearrange("(c n) -> c n", n=NT))
         ori_u8 = keep.tile([P, D], U8, name="ori_u8")
         nc.sync.dma_start(out=ori_u8[:], in_=ori_bytes)
         ori_s = keep.tile([P, G1, 4], F32, name="ori_s")
         nc.sync.dma_start(out=ori_s[:], in_=ori_scale.rearrange("o (g p t) -> p (o g) t", p=P, t=4))
-        for q in range(4):
-            nc.sync.dma_start(
-                out=s1[32 * q : 32 * q + 16, :].bitcast(I32), in_=W1_scales[:, 4 * q : 4 * q + 4, :].bitcast(I32)
-            )
+        node = keep.tile([P, D], BF16, name="node")
+        nc.sync.dma_start(out=node[:], in_=node_embed)
+
+        def load_scales(plane, scales, g0, n0, n1):
+            for q in (2, 3, 0, 1):
+                nc.sync.dma_start(
+                    out=plane[32 * q : 32 * q + 16, :].bitcast(I32),
+                    in_=scales[g0 : g0 + 4, 4 * q : 4 * q + 4, n0:n1].bitcast(I32),
+                )
 
         def load_words(words, name, g0, g1, n0, n1):
             t = keep.tile([P, g1 - g0, n1 - n0], U32, name=name, align_bytes=256)
@@ -74,31 +74,34 @@ def tile_node_interaction_w_w8_kernel(
             nc.sync.dma_start(out=t[:].bitcast(I32), in_=src)
             return {g: t[:, g - g0, :] for g in range(g0, g1)}
 
-        w1 = []
+        def load_w2(n, g0):
+            w2[n].update(load_words(W2_words, "w2_%d_%d" % (n, g0), g0, g0 + 2, n * NT, (n + 1) * NT))
+
+        load_scales(s1[0], W1_scales, 0, 0, 2 * NT)
+        w1 = [{} for c in range(C1)]
+        w2 = [{} for n in range(C2 - 1)]
         gate = []
         for c in range(C1):
-            cw = {}
-            for g0 in range(0, G1, 2):
-                cw.update(load_words(W1_words, "w1_%d_%d" % (c, g0), g0, g0 + 2, c * NT, (c + 1) * NT))
-            w1.append(cw)
+            w1[c].update(load_words(W1_words, "w1_%d_0" % c, 0, 2, c * NT, (c + 1) * NT))
+            if c % 2 == 1 and c + 1 < C1:
+                load_scales(s1[(c + 1) // 2], W1_scales, 0, (c + 1) * NT, (c + 3) * NT)
+            w1[c].update(load_words(W1_words, "w1_%d_2" % c, 2, 4, c * NT, (c + 1) * NT))
             if c % 2 == 0:
                 xe = keep.tile([P, 2 * NT], BF16, name="gate%d" % c)
                 nc.sync.dma_start(out=xe[:], in_=x_edge_c[:, c * NT : (c + 2) * NT])
                 gate.extend([xe[:, 0:NT], xe[:, NT : 2 * NT]])
             if c == 0:
                 nc.sync.dma_start(out=b2_rows[0:C2, :], in_=b2.rearrange("(c n) -> c n", n=NT))
-        for i in range(2):
-            for q in range(4):
-                nc.sync.dma_start(
-                    out=s2[i][32 * q : 32 * q + 16, :].bitcast(I32),
-                    in_=W2_scales[4 * i : 4 * i + 4, 4 * q : 4 * q + 4, :].bitcast(I32),
-                )
-        w2 = []
-        for n in range(C2 - 1):
-            cw = {}
-            for g0 in range(0, G2, 2):
-                cw.update(load_words(W2_words, "w2_%d_%d" % (n, g0), g0, g0 + 2, n * NT, (n + 1) * NT))
-            w2.append(cw)
+            if c % 4 == 3:
+                load_scales(s2[c // 4], W2_scales, 4 * (c // 4), 0, D)
+            if c % 2 == 1 and c >= 3:
+                load_w2(0, c - 3)
+        for g0 in range(0, G2 - 2, 2):
+            load_w2(1, g0)
+        load_w2(0, G2 - 2)
+        load_w2(1, G2 - 2)
+        for g0 in range(0, G2, 2):
+            load_w2(2, g0)
         n0 = (C2 - 1) * NT
         half = NT // 2
         wide = {}
@@ -143,36 +146,24 @@ def tile_node_interaction_w_w8_kernel(
             nc.vector.quantize_mx(out=codes[:].bitcast(FP8X4), scales=scales[:], in_=src)
             return codes, scales
 
-        ps_b = spread_matmuls(b1_rows, 0, 6)
-        copy_bias1(ps_b, 0)
-
-        node_words = node[:].bitcast(F32)
-        node_t = []
-        for pair in range(2):
-            ps = bank(4 + pair, [P, 2, 2, P], F32)
-            for i in range(2):
-                g = 2 * pair + i
-                for u in range(2):
-                    nc.tensor.transpose(ps[:, i, u, :], node_words[:, 256 * g + u : 256 * (g + 1) : 2], ident[:])
-            node_t.append(ps)
         ori_wide = []
         for g in range(G1):
             t = keep.tile([P, KP], BF16, name="ori_wide%d" % g)
-            nc.vector.tensor_copy(
-                out=t[:].rearrange("p (u m e) -> p m u e", u=2, e=2),
-                in_=ori_u8[:, g * KP : (g + 1) * KP].bitcast(FP8).rearrange("p (m u e) -> p m u e", u=2, e=2),
-            )
+            codes = ori_u8[:, g * KP : (g + 1) * KP].bitcast(FP8)
+            if g < 2:
+                nc.vector.tensor_copy(
+                    out=t[:].rearrange("p (u m e) -> p m u e", u=2, e=2),
+                    in_=codes.rearrange("p (m u e) -> p m u e", u=2, e=2),
+                )
+            else:
+                nc.scalar.copy(
+                    out=t[:].rearrange("p (u m e) -> p u m e", u=2, e=2),
+                    in_=codes.rearrange("p (m u e) -> p u m e", u=2, e=2),
+                )
             ori_wide.append(t)
-        for g in range(G1):
-            xg = work.tile([P, 4 * P], BF16, name="xg", tag="xg", bufs=4, align_bytes=64)
-            nc.scalar.copy(
-                out=xg[:].bitcast(F32).rearrange("p (r u) -> p r u", u=2),
-                in_=node_t[g // 2][:, g % 2, :, :].rearrange("p u r -> p r u"),
-            )
-            xq[g, 0] = quantize(xg[:], "xq%d_0" % g, P)
 
-        ps_b = spread_matmuls(b1_rows, 1, 7)
-        copy_bias1(ps_b, 1)
+        for pair in range(2):
+            copy_bias1(spread_matmuls(b1_rows, pair, 6 + pair), pair)
 
         ori_t = []
         for pair in range(2):
@@ -182,18 +173,40 @@ def tile_node_interaction_w_w8_kernel(
                 for u in range(2):
                     nc.tensor.transpose(ps[:, i, u, :], words[:, P * u : P * (u + 1)], ident[:])
             ori_t.append(ps)
-        scaled = []
-        for g in range(G1 + 1):
-            if g < G1:
-                xg = work.tile([P, 4 * P], BF16, name="xg", tag="xg", bufs=4, align_bytes=64)
-                src = ori_t[g // 2][:, g % 2, :, :].bitcast(BF16).rearrange("p u (r e) -> p r u e", e=2)
-                fac = ori_s[:, g, :].rearrange("p (u e) -> p u e", u=2).unsqueeze(1).to_broadcast([P, P, 2, 2])
-                nc.vector.tensor_tensor(
-                    out=xg[:].rearrange("p (r u e) -> p r u e", u=2, e=2), in0=src, in1=fac, op=MULT
-                )
-                scaled.append(xg)
-            if g > 0:
-                xq[g - 1, 1] = quantize(scaled[g - 1][:], "xq%d_1" % (g - 1), P)
+        node_words = node[:].bitcast(F32)
+        node_t = []
+        for pair in range(2):
+            ps = bank(4 + pair, [P, 2, 2, P], F32)
+            for i in range(2):
+                g = 2 * pair + i
+                for u in range(2):
+                    nc.tensor.transpose(ps[:, i, u, :], node_words[:, 256 * g + u : 256 * (g + 1) : 2], ident[:])
+            node_t.append(ps)
+
+        x_grouped = {}
+        for g in range(G1):
+            xg = work.tile([P, 4 * P], BF16, name="xg_node", tag="xg_node", bufs=4, align_bytes=64)
+            nc.scalar.copy(
+                out=xg[:].bitcast(F32).rearrange("p (r u) -> p r u", u=2),
+                in_=node_t[g // 2][:, g % 2, :, :].rearrange("p u r -> p r u"),
+            )
+            x_grouped[g, 0] = xg
+
+        def scale_ori(g):
+            xg = work.tile([P, 4 * P], BF16, name="xg_ori", tag="xg_ori", bufs=2, align_bytes=64)
+            src = ori_t[g // 2][:, g % 2, :, :].bitcast(BF16).rearrange("p u (r e) -> p r u e", e=2)
+            fac = ori_s[:, g, :].rearrange("p (u e) -> p u e", u=2).unsqueeze(1).to_broadcast([P, P, 2, 2])
+            nc.vector.tensor_tensor(out=xg[:].rearrange("p (r u e) -> p r u e", u=2, e=2), in0=src, in1=fac, op=MULT)
+            x_grouped[g, 1] = xg
+
+        for g0, order in ((0, (1, 0)), (2, (0, 1))):
+            scale_ori(g0)
+            scale_ori(g0 + 1)
+            for j in order:
+                for g in (g0, g0 + 1):
+                    xq[g, j] = quantize(x_grouped[g, j][:], "xq%d_%d" % (g, j), P)
+
+        copy_bias1(spread_matmuls(b1_rows, 2, 6), 2)
 
         def mx(acc, stat, j, words, scale_plane, first, last):
             codes, scales = stat
@@ -214,10 +227,11 @@ def tile_node_interaction_w_w8_kernel(
 
         def stage1_matmuls(c):
             acc = [bank((2 * c + j) % 4, [P, NT], F32) for j in range(2)]
-            for g0 in range(0, G1, 2):
-                for j in range(2):
+            cols = slice((c % 2) * NT, (c % 2 + 1) * NT)
+            for g0, order in ((0, (1, 0)), (2, (0, 1))):
+                for j in order:
                     for g in (g0, g0 + 1):
-                        mx(acc[j][:], xq[g, j], 0, w1[c][g], s1[4 * g : P, c * NT : (c + 1) * NT], g == 0, g == G1 - 1)
+                        mx(acc[j][:], xq[g, j], 0, w1[c][g], s1[c // 2][4 * g : P, cols], g == 0, g == G1 - 1)
             return acc
 
         def bias_silu(acc, bias, permute):
@@ -267,32 +281,6 @@ def tile_node_interaction_w_w8_kernel(
         def quantize_h(c):
             hq[c] = quantize(h_grouped[c][:], "hq%d" % c, 2 * P)
 
-        for c in range(C1):
-            acc = stage1_matmuls(c)
-            spread = []
-            if c == 0:
-                spread = [spread_matmuls(b1_rows, 2, 6), spread_matmuls(b1_rows, 3, 7)]
-            if c == 1:
-                spread = [spread_matmuls(b2_rows, 0, 6), spread_matmuls(b2_rows, 1, 7)]
-            if c >= 3 and c % 2 == 1:
-                transpose_h(c - 3)
-                transpose_h(c - 2)
-            acts = [bias_silu(acc[j][:], bias1[c], True) for j in range(2)]
-            for i, ps in enumerate(spread):
-                if c == 0:
-                    copy_bias1(ps, 2 + i)
-                else:
-                    copy_bias2(ps, i)
-            if c >= 4:
-                quantize_h(c - 4)
-            if c >= 3 and c % 2 == 1:
-                copy_h(c - 3, False)
-                copy_h(c - 2, False)
-            for j in range(2):
-                apply_gate(c, j, acts[j])
-        quantize_h(4)
-        quantize_h(5)
-
         def stage2_pass(acc, g, words, n0, n1):
             for j in range(2):
                 mx(acc[j][:], hq[g], j, words, s2[g // 4][4 * (g % 4) : P, n0:n1], g == 0, g == G2 - 1)
@@ -303,18 +291,54 @@ def tile_node_interaction_w_w8_kernel(
             nc.vector.tensor_tensor(out=res[:], in0=acts[0][:], in1=acts[1][:], op=ADD)
             nc.sync.dma_start(out=out2d[:, n0:n1], in_=res[:])
 
-        for n in range(C2 - 1):
-            acc = [bank((6 + 2 * n + j) % 8, [P, NT], F32) for j in range(2)]
-            for g in range(G2):
-                if n == 0 and g == 4:
-                    transpose_h(6)
-                    transpose_h(7)
-                    copy_h(6, False)
-                    copy_h(7, True)
-                    quantize_h(6)
-                    quantize_h(7)
-                stage2_pass(acc, g, w2[n][g], n * NT, (n + 1) * NT)
-            finish(acc, bias2[n], n * NT, (n + 1) * NT, "res%d" % n)
+        acc2 = {}
+
+        def stage2_passes(n, g0, g1):
+            if g0 == 0:
+                acc2[n] = [bank((6 + 2 * n + j) % 8, [P, NT], F32) for j in range(2)]
+            for g in range(g0, g1):
+                stage2_pass(acc2[n], g, w2[n][g], n * NT, (n + 1) * NT)
+
+        for c in range(C1):
+            acc = stage1_matmuls(c)
+            if c == 0:
+                ps1 = spread_matmuls(b1_rows, 3, 7)
+                ps2 = spread_matmuls(b2_rows, 0, 6)
+            if c == 1:
+                ps2 = spread_matmuls(b2_rows, 1, 7)
+            if c >= 2 and c % 2 == 0:
+                transpose_h(c - 2)
+                transpose_h(c - 1)
+            if c >= 3 and c % 2 == 1:
+                stage2_passes(0, c - 3, c - 1)
+            acts = [bias_silu(acc[j][:], bias1[c], True) for j in range(2)]
+            if c == 0:
+                copy_bias1(ps1, 3)
+            if c <= 1:
+                copy_bias2(ps2, c)
+            if c >= 2 and c % 2 == 0:
+                copy_h(c - 2, False)
+                copy_h(c - 1, False)
+            for j in range(2):
+                apply_gate(c, j, acts[j])
+            if c >= 2 and c % 2 == 0:
+                quantize_h(c - 2)
+                quantize_h(c - 1)
+
+        stage2_passes(1, 0, 2)
+        transpose_h(6)
+        transpose_h(7)
+        copy_h(6, False)
+        copy_h(7, True)
+        quantize_h(6)
+        quantize_h(7)
+        stage2_passes(1, 2, 6)
+        stage2_passes(0, 6, 8)
+        finish(acc2[0], bias2[0], 0, NT, "res0")
+        stage2_passes(1, 6, 8)
+        finish(acc2[1], bias2[1], NT, 2 * NT, "res1")
+        stage2_passes(2, 0, 8)
+        finish(acc2[2], bias2[2], 2 * NT, 3 * NT, "res2")
         acc_a = [bank(4 + j, [P, half], F32) for j in range(2)]
         acc_b = [bank(6 + j, [P, half], F32) for j in range(2)]
         for g in range(4):

@@ -46,14 +46,18 @@ def tile_node_interaction_w_w8_kernel(
         make_identity(nc, ident[:])
         b1_rows = keep.tile([P, NT], BF16, name="b1_rows")
         b2_rows = keep.tile([P, NT], BF16, name="b2_rows")
-        s1 = [keep.tile([P, 2 * NT], U8, name="s1_%d" % i, align_bytes=64) for i in range(C1 // 2)]
+        s1_first = keep.tile([P, 2 * NT], U8, name="s1_first", align_bytes=64)
+        s1_rest = keep.tile([P, H - 2 * NT], U8, name="s1_rest", align_bytes=64)
+        s1 = [s1_first[:, c * NT : (c + 1) * NT] for c in range(2)]
+        s1 = s1 + [s1_rest[:, c * NT : (c + 1) * NT] for c in range(C1 - 2)]
         s2 = [keep.tile([P, D], U8, name="s2_%d" % i, align_bytes=64) for i in range(2)]
-        for t in [b1_rows] + s1 + [b2_rows] + s2:
+        for t in [b1_rows, b2_rows, s1_rest] + s2 + [s1_first]:
             nc.vector.memset(t[:].bitcast(I32), 0)
         pick = keep.tile([P, C1], BF16, name="pick")
         nc.vector.tensor_copy(out=pick[:], in_=ident[:, 0:C1])
 
         nc.scalar.dma_start(out=b1_rows[0:C1, :], in_=b1.rearrange("(c n) -> c n", n=NT))
+        nc.scalar.dma_start(out=b2_rows[0:C2, :], in_=b2.rearrange("(c n) -> c n", n=NT))
         ori_u8 = keep.tile([P, D], U8, name="ori_u8")
         nc.sync.dma_start(out=ori_u8[:], in_=ori_bytes)
         ori_s = keep.tile([P, G1, 4], F32, name="ori_s")
@@ -77,23 +81,20 @@ def tile_node_interaction_w_w8_kernel(
         def load_w2(n, g0):
             w2[n].update(load_words(W2_words, "w2_%d_%d" % (n, g0), g0, g0 + 2, n * NT, (n + 1) * NT))
 
-        load_scales(s1[0], W1_scales, 0, 0, 2 * NT)
+        load_scales(s1_rest, W1_scales, 0, 2 * NT, H)
+        for i in range(2):
+            load_scales(s2[i], W2_scales, 4 * i, 0, D)
+        load_scales(s1_first, W1_scales, 0, 0, 2 * NT)
         w1 = [{} for c in range(C1)]
         w2 = [{} for n in range(C2 - 1)]
         gate = []
         for c in range(C1):
             w1[c].update(load_words(W1_words, "w1_%d_0" % c, 0, 2, c * NT, (c + 1) * NT))
-            if c % 2 == 1 and c + 1 < C1:
-                load_scales(s1[(c + 1) // 2], W1_scales, 0, (c + 1) * NT, (c + 3) * NT)
             w1[c].update(load_words(W1_words, "w1_%d_2" % c, 2, 4, c * NT, (c + 1) * NT))
             if c % 2 == 0:
                 xe = keep.tile([P, 2 * NT], BF16, name="gate%d" % c)
                 nc.sync.dma_start(out=xe[:], in_=x_edge_c[:, c * NT : (c + 2) * NT])
                 gate.extend([xe[:, 0:NT], xe[:, NT : 2 * NT]])
-            if c == 0:
-                nc.sync.dma_start(out=b2_rows[0:C2, :], in_=b2.rearrange("(c n) -> c n", n=NT))
-            if c % 4 == 3:
-                load_scales(s2[c // 4], W2_scales, 4 * (c // 4), 0, D)
             if c % 2 == 1 and c >= 3:
                 load_w2(0, c - 3)
         for g0 in range(0, G2 - 2, 2):
@@ -206,7 +207,10 @@ def tile_node_interaction_w_w8_kernel(
                 for g in (g0, g0 + 1):
                     xq[g, j] = quantize(x_grouped[g, j][:], "xq%d_%d" % (g, j), P)
 
-        copy_bias1(spread_matmuls(b1_rows, 2, 6), 2)
+        for pair in range(2, C1 // 2):
+            copy_bias1(spread_matmuls(b1_rows, pair, 4 + pair), pair)
+        for pair in range(C2 // 2):
+            copy_bias2(spread_matmuls(b2_rows, pair, 4 + pair), pair)
 
         def mx(acc, stat, j, words, scale_plane, first, last):
             codes, scales = stat
@@ -227,11 +231,10 @@ def tile_node_interaction_w_w8_kernel(
 
         def stage1_matmuls(c):
             acc = [bank((2 * c + j) % 4, [P, NT], F32) for j in range(2)]
-            cols = slice((c % 2) * NT, (c % 2 + 1) * NT)
             for g0, order in ((0, (1, 0)), (2, (0, 1))):
                 for j in order:
                     for g in (g0, g0 + 1):
-                        mx(acc[j][:], xq[g, j], 0, w1[c][g], s1[c // 2][4 * g : P, cols], g == 0, g == G1 - 1)
+                        mx(acc[j][:], xq[g, j], 0, w1[c][g], s1[c][4 * g : P, :], g == 0, g == G1 - 1)
             return acc
 
         def bias_silu(acc, bias, permute):
@@ -301,21 +304,12 @@ def tile_node_interaction_w_w8_kernel(
 
         for c in range(C1):
             acc = stage1_matmuls(c)
-            if c == 0:
-                ps1 = spread_matmuls(b1_rows, 3, 7)
-                ps2 = spread_matmuls(b2_rows, 0, 6)
-            if c == 1:
-                ps2 = spread_matmuls(b2_rows, 1, 7)
             if c >= 2 and c % 2 == 0:
                 transpose_h(c - 2)
                 transpose_h(c - 1)
             if c >= 3 and c % 2 == 1:
                 stage2_passes(0, c - 3, c - 1)
             acts = [bias_silu(acc[j][:], bias1[c], True) for j in range(2)]
-            if c == 0:
-                copy_bias1(ps1, 3)
-            if c <= 1:
-                copy_bias2(ps2, c)
             if c >= 2 and c % 2 == 0:
                 copy_h(c - 2, False)
                 copy_h(c - 1, False)

@@ -58,11 +58,11 @@ def tile_node_interaction_w_w8_kernel(
 
         nc.scalar.dma_start(out=b1_rows[0:C1, :], in_=b1.rearrange("(c n) -> c n", n=NT))
         nc.scalar.dma_start(out=b2_rows[0:C2, :], in_=b2.rearrange("(c n) -> c n", n=NT))
-        ori_u8 = keep.tile([P, D], U8, name="ori_u8")
+        ori_u8 = keep.tile([P, D], U8, name="ori_u8", align_bytes=256)
         nc.sync.dma_start(out=ori_u8[:], in_=ori_bytes)
         ori_s = keep.tile([P, G1, 4], F32, name="ori_s")
         nc.sync.dma_start(out=ori_s[:], in_=ori_scale.rearrange("o (g p t) -> p (o g) t", p=P, t=4))
-        node = keep.tile([P, D], BF16, name="node")
+        node = keep.tile([P, D], BF16, name="node", align_bytes=256)
         nc.sync.dma_start(out=node[:], in_=node_embed)
 
         def load_scales(plane, scales, g0, n0, n1):
@@ -78,41 +78,42 @@ def tile_node_interaction_w_w8_kernel(
             nc.sync.dma_start(out=t[:].bitcast(I32), in_=src)
             return {g: t[:, g - g0, :] for g in range(g0, g1)}
 
-        def load_w2(n, g0):
-            w2[n].update(load_words(W2_words, "w2_%d_%d" % (n, g0), g0, g0 + 2, n * NT, (n + 1) * NT))
-
         load_scales(s1_rest, W1_scales, 0, 2 * NT, H)
         for i in range(2):
             load_scales(s2[i], W2_scales, 4 * i, 0, D)
         load_scales(s1_first, W1_scales, 0, 0, 2 * NT)
+        def split(target, first, loaded):
+            for g, words in loaded.items():
+                for i in range(words.shape[1] // NT):
+                    target[first + i][g] = words[:, i * NT : (i + 1) * NT]
+
         w1 = [{} for c in range(C1)]
-        w2 = [{} for n in range(C2 - 1)]
+        w2 = [{} for n in range(C2)]
         gate = []
-        for c in range(C1):
-            w1[c].update(load_words(W1_words, "w1_%d_0" % c, 0, 2, c * NT, (c + 1) * NT))
-            w1[c].update(load_words(W1_words, "w1_%d_2" % c, 2, 4, c * NT, (c + 1) * NT))
-            if c % 2 == 0:
-                xe = keep.tile([P, 2 * NT], BF16, name="gate%d" % c)
-                nc.sync.dma_start(out=xe[:], in_=x_edge_c[:, c * NT : (c + 2) * NT])
-                gate.extend([xe[:, 0:NT], xe[:, NT : 2 * NT]])
-            if c % 2 == 1 and c >= 3:
-                load_w2(0, c - 3)
-        for g0 in range(0, G2 - 2, 2):
-            load_w2(1, g0)
-        load_w2(0, G2 - 2)
-        load_w2(1, G2 - 2)
-        for g0 in range(0, G2, 2):
-            load_w2(2, g0)
+        for c in range(0, C1, 2):
+            for g in range(G1):
+                split(w1, c, load_words(W1_words, "w1_%d_%d" % (c, g), g, g + 1, c * NT, (c + 2) * NT))
+            if c == 4:
+                split(w2, 0, load_words(W2_words, "w2_early", 0, 2, 0, NT))
+            if c % 4 == 0:
+                xe = keep.tile([P, 4 * NT], BF16, name="gate%d" % c, align_bytes=256)
+                nc.sync.dma_start(out=xe[:], in_=x_edge_c[:, c * NT : (c + 4) * NT])
+                gate.extend([xe[:, i * NT : (i + 1) * NT] for i in range(4)])
+        split(w2, 1, load_words(W2_words, "w2_catch_up", 0, 2, NT, 2 * NT))
+        for g in range(2, G2):
+            split(w2, 0, load_words(W2_words, "w2_low_%d" % g, g, g + 1, 0, 2 * NT))
+        for g in range(2):
+            split(w2, 2, load_words(W2_words, "w2_high_%d" % g, g, g + 1, 2 * NT, 4 * NT))
+        for n, g_end in ((2, G2), (3, G2 - 2)):
+            for g in range(2, g_end, 2):
+                split(w2, n, load_words(W2_words, "w2_%d_%d" % (n, g), g, g + 2, n * NT, (n + 1) * NT))
         n0 = (C2 - 1) * NT
         half = NT // 2
-        wide = {}
-        for g0 in (0, 2):
-            wide.update(load_words(W2_words, "w2_last_%d" % g0, g0, g0 + 2, n0, n0 + NT))
-        w2a = {g: wide[g][:, 0:half] for g in wide}
-        w2b = {g: wide[g][:, half:NT] for g in wide}
-        w2a.update(load_words(W2_words, "w2_a", 4, 8, n0, n0 + half))
-        for g0, g1 in ((4, 6), (6, 7), (7, 8)):
-            w2b.update(load_words(W2_words, "w2_b%d" % g0, g0, g1, n0 + half, n0 + NT))
+        w2a = {g: w2[3][g][:, 0:half] for g in range(G2 - 2)}
+        w2b = {g: w2[3][g][:, half:NT] for g in range(G2 - 2)}
+        w2a.update(load_words(W2_words, "w2_a", G2 - 2, G2, n0, n0 + half))
+        for g in range(G2 - 2, G2):
+            w2b.update(load_words(W2_words, "w2_b%d" % g, g, g + 1, n0 + half, n0 + NT))
 
         bias1 = []
         bias2 = []
@@ -209,8 +210,6 @@ def tile_node_interaction_w_w8_kernel(
 
         for pair in range(2, C1 // 2):
             copy_bias1(spread_matmuls(b1_rows, pair, 4 + pair), pair)
-        for pair in range(C2 // 2):
-            copy_bias2(spread_matmuls(b2_rows, pair, 4 + pair), pair)
 
         def mx(acc, stat, j, words, scale_plane, first, last):
             codes, scales = stat
@@ -229,17 +228,16 @@ def tile_node_interaction_w_w8_kernel(
         h_grouped = {}
         hq = {}
 
-        def stage1_matmuls(c):
-            acc = [bank((2 * c + j) % 4, [P, NT], F32) for j in range(2)]
-            for g0, order in ((0, (1, 0)), (2, (0, 1))):
-                for j in order:
-                    for g in (g0, g0 + 1):
-                        mx(acc[j][:], xq[g, j], 0, w1[c][g], s1[c][4 * g : P, :], g == 0, g == G1 - 1)
+        def stage1_matmuls(c0):
+            acc = {(c, j): bank(2 * (c - c0) + j, [P, NT], F32) for c in (c0, c0 + 1) for j in range(2)}
+            for g in range(G1):
+                for c, j in acc:
+                    mx(acc[c, j][:], xq[g, j], 0, w1[c][g], s1[c][4 * g : P, :], g == 0, g == G1 - 1)
             return acc
 
         def bias_silu(acc, bias, permute):
             width = acc.shape[1]
-            pre = work.tile([P, width], F32, name="pre", tag="pre")
+            pre = work.tile([P, width], F32, name="pre", tag="pre", bufs=4)
             if permute:
                 nc.vector.tensor_tensor(
                     out=pre[:].rearrange("p (u m e) -> p u m e", u=2, e=2),
@@ -254,7 +252,7 @@ def tile_node_interaction_w_w8_kernel(
             return act
 
         def apply_gate(c, j, act):
-            t = work.tile([P, NT], BF16, name="h", tag="h", bufs=8)
+            t = work.tile([P, NT], BF16, name="h", tag="h", bufs=4)
             nc.vector.tensor_tensor(
                 out=t[:].rearrange("p (u m e) -> p u m e", u=2, e=2),
                 in0=act[:].rearrange("p (u m e) -> p u m e", u=2, e=2),
@@ -288,59 +286,73 @@ def tile_node_interaction_w_w8_kernel(
             for j in range(2):
                 mx(acc[j][:], hq[g], j, words, s2[g // 4][4 * (g % 4) : P, n0:n1], g == 0, g == G2 - 1)
 
-        def finish(acc, bias, n0, n1, name):
-            acts = [bias_silu(acc[j][:], bias, False) for j in range(2)]
-            res = keep.tile([P, n1 - n0], F32, name=name)
+        def activate(acc, bias):
+            return [bias_silu(acc[j][:], bias, False) for j in range(2)]
+
+        def add_and_store(acts, n0, n1, name):
+            res = keep.tile([P, n1 - n0], F32, name=name, align_bytes=256)
             nc.vector.tensor_tensor(out=res[:], in0=acts[0][:], in1=acts[1][:], op=ADD)
             nc.sync.dma_start(out=out2d[:, n0:n1], in_=res[:])
 
         acc2 = {}
 
-        def stage2_passes(n, g0, g1):
-            if g0 == 0:
-                acc2[n] = [bank((6 + 2 * n + j) % 8, [P, NT], F32) for j in range(2)]
+        def stage2_passes(groups, g0, g1):
             for g in range(g0, g1):
-                stage2_pass(acc2[n], g, w2[n][g], n * NT, (n + 1) * NT)
+                for n in groups:
+                    if g == 0:
+                        acc2[n] = [bank((6 + 2 * n + j) % 8, [P, NT], F32) for j in range(2)]
+                    stage2_pass(acc2[n], g, w2[n][g], n * NT, (n + 1) * NT)
 
-        for c in range(C1):
-            acc = stage1_matmuls(c)
-            if c >= 2 and c % 2 == 0:
-                transpose_h(c - 2)
-                transpose_h(c - 1)
-            if c >= 3 and c % 2 == 1:
-                stage2_passes(0, c - 3, c - 1)
-            acts = [bias_silu(acc[j][:], bias1[c], True) for j in range(2)]
-            if c >= 2 and c % 2 == 0:
-                copy_h(c - 2, False)
-                copy_h(c - 1, False)
-            for j in range(2):
-                apply_gate(c, j, acts[j])
-            if c >= 2 and c % 2 == 0:
-                quantize_h(c - 2)
-                quantize_h(c - 1)
+        for c0 in range(0, C1, 2):
+            acc = stage1_matmuls(c0)
+            if c0 == 0:
+                spread = [spread_matmuls(b2_rows, pair, 4 + pair) for pair in range(C2 // 2)]
+            else:
+                transpose_h(c0 - 2)
+                transpose_h(c0 - 1)
+            if c0 == 4:
+                stage2_passes([0], 0, 2)
+            acts = {(c, j): bias_silu(acc[c, j][:], bias1[c], True) for c, j in acc}
+            if c0 == 0:
+                for pair, ps in enumerate(spread):
+                    copy_bias2(ps, pair)
+            else:
+                copy_h(c0 - 2, False)
+                copy_h(c0 - 1, False)
+            for c, j in acts:
+                apply_gate(c, j, acts[c, j])
+            if c0 > 0:
+                quantize_h(c0 - 2)
+                quantize_h(c0 - 1)
 
-        stage2_passes(1, 0, 2)
+        stage2_passes([1], 0, 2)
+        stage2_passes([0, 1], 2, 4)
         transpose_h(6)
         transpose_h(7)
         copy_h(6, False)
         copy_h(7, True)
         quantize_h(6)
         quantize_h(7)
-        stage2_passes(1, 2, 6)
-        stage2_passes(0, 6, 8)
-        finish(acc2[0], bias2[0], 0, NT, "res0")
-        stage2_passes(1, 6, 8)
-        finish(acc2[1], bias2[1], NT, 2 * NT, "res1")
-        stage2_passes(2, 0, 8)
-        finish(acc2[2], bias2[2], 2 * NT, 3 * NT, "res2")
+        stage2_passes([0, 1], 4, G2)
+        acts_low = [activate(acc2[n], bias2[n]) for n in range(2)]
+        for n in range(2):
+            add_and_store(acts_low[n], n * NT, (n + 1) * NT, "res%d" % n)
         acc_a = [bank(4 + j, [P, half], F32) for j in range(2)]
         acc_b = [bank(6 + j, [P, half], F32) for j in range(2)]
-        for g in range(4):
+        for g in range(2):
+            stage2_passes([2], g, g + 1)
             stage2_pass(acc_a, g, w2a[g], n0, n0 + half)
             stage2_pass(acc_b, g, w2b[g], n0 + half, n0 + NT)
-        for g in range(4, G2):
+        stage2_passes([2], 2, G2)
+        add_and_store(activate(acc2[2], bias2[2]), 2 * NT, 3 * NT, "res2")
+        for g in range(2, G2 - 2):
             stage2_pass(acc_a, g, w2a[g], n0, n0 + half)
-        finish(acc_a, bias2[C2 - 1][:, 0:half], n0, n0 + half, "res_a")
-        for g in range(4, G2):
             stage2_pass(acc_b, g, w2b[g], n0 + half, n0 + NT)
-        finish(acc_b, bias2[C2 - 1][:, half:NT], n0 + half, n0 + NT, "res_b")
+        for g in range(G2 - 2, G2):
+            stage2_pass(acc_a, g, w2a[g], n0, n0 + half)
+        acts_a = activate(acc_a, bias2[C2 - 1][:, 0:half])
+        for g in range(G2 - 2, G2):
+            stage2_pass(acc_b, g, w2b[g], n0 + half, n0 + NT)
+        acts_b = activate(acc_b, bias2[C2 - 1][:, half:NT])
+        add_and_store(acts_a, n0, n0 + half, "res_a")
+        add_and_store(acts_b, n0 + half, n0 + NT, "res_b")

from contextlib import ExitStack

import concourse.mybir as mybir
from concourse.masks import make_identity

E, D, H = 128, 2048, 4096
FLOPS = 2 * (2 * E) * D * H * 2

F32 = mybir.dt.float32
BF16 = mybir.dt.bfloat16
I32 = mybir.dt.int32
U32 = mybir.dt.uint32
U8 = mybir.dt.uint8
FP8 = mybir.dt.float8_e4m3fn
FP8X4 = mybir.dt.float8_e4m3fn_x4
ADD = mybir.AluOpType.add
MULT = mybir.AluOpType.mult
SILU = mybir.ActivationFunctionType.Silu

P = 128
KP = 512
NT = 512
G1 = D // KP
G2 = H // KP
C1 = H // NT
C2 = D // NT


def tile_node_interaction_w_w8_kernel(
    tc, node_embed, x_edge_c, ori_bytes, ori_scale, W1_words, W1_scales, b1, W2_words, W2_scales, b2, edge_num, out
):
    nc = tc.nc
    assert edge_num == E
    out2d = out.rearrange("e a c -> e (a c)")

    with ExitStack() as ctx:
        keep = ctx.enter_context(tc.tile_pool(name="keep", bufs=1))
        work = ctx.enter_context(tc.tile_pool(name="work", bufs=3))
        psum = ctx.enter_context(tc.psum_pool(name="psum", bufs=1))
        ctx.enter_context(tc.manual_schedule())

        def bank(i, shape, dtype):
            return psum.tile(shape, dtype, name="bank%d" % i, tag="bank%d" % i)

        ident = keep.tile([P, P], F32, name="ident")
        make_identity(nc, ident[:])
        b1_rows = keep.tile([P, NT], BF16, name="b1_rows")
        b2_rows = keep.tile([P, NT], BF16, name="b2_rows")
        s1_first = keep.tile([P, 2 * NT], U8, name="s1_first", align_bytes=64)
        s1_rest = keep.tile([P, H - 2 * NT], U8, name="s1_rest", align_bytes=64)
        s1 = [s1_first[:, c * NT : (c + 1) * NT] for c in range(2)]
        s1 = s1 + [s1_rest[:, c * NT : (c + 1) * NT] for c in range(C1 - 2)]
        s2 = [keep.tile([P, D], U8, name="s2_%d" % i, align_bytes=64) for i in range(2)]
        for t in [b1_rows, b2_rows, s1_rest] + s2 + [s1_first]:
            nc.vector.memset(t[:].bitcast(I32), 0)
        pick = keep.tile([P, C1], BF16, name="pick")
        nc.vector.tensor_copy(out=pick[:], in_=ident[:, 0:C1])

        nc.scalar.dma_start(out=b1_rows[0:C1, :], in_=b1.rearrange("(c n) -> c n", n=NT))
        nc.scalar.dma_start(out=b2_rows[0:C2, :], in_=b2.rearrange("(c n) -> c n", n=NT))
        ori_u8 = keep.tile([P, D], U8, name="ori_u8", align_bytes=256)
        nc.sync.dma_start(out=ori_u8[:], in_=ori_bytes)
        ori_s = keep.tile([P, G1, 4], F32, name="ori_s")
        nc.sync.dma_start(out=ori_s[:], in_=ori_scale.rearrange("o (g p t) -> p (o g) t", p=P, t=4))
        node = keep.tile([P, D], BF16, name="node", align_bytes=256)
        nc.sync.dma_start(out=node[:], in_=node_embed)

        def load_scales(plane, scales, g0, n0, n1):
            for q in (2, 3, 0, 1):
                nc.sync.dma_start(
                    out=plane[32 * q : 32 * q + 16, :].bitcast(I32),
                    in_=scales[g0 : g0 + 4, 4 * q : 4 * q + 4, n0:n1].bitcast(I32),
                )

        def load_words(words, name, g0, g1, n0, n1):
            t = keep.tile([P, g1 - g0, n1 - n0], U32, name=name, align_bytes=256)
            src = words[g0:g1].rearrange("g p n t -> p g (n t)")[:, :, 4 * n0 : 4 * n1].bitcast(I32)
            nc.sync.dma_start(out=t[:].bitcast(I32), in_=src)
            return {g: t[:, g - g0, :] for g in range(g0, g1)}

        load_scales(s1_rest, W1_scales, 0, 2 * NT, H)
        for i in range(2):
            load_scales(s2[i], W2_scales, 4 * i, 0, D)
        load_scales(s1_first, W1_scales, 0, 0, 2 * NT)
        def split(target, first, loaded):
            for g, words in loaded.items():
                for i in range(words.shape[1] // NT):
                    target[first + i][g] = words[:, i * NT : (i + 1) * NT]

        w1 = [{} for c in range(C1)]
        w2 = [{} for n in range(C2)]
        gate = []
        for c in range(0, C1, 2):
            for g in range(G1):
                split(w1, c, load_words(W1_words, "w1_%d_%d" % (c, g), g, g + 1, c * NT, (c + 2) * NT))
            if c == 4:
                split(w2, 0, load_words(W2_words, "w2_early", 0, 2, 0, NT))
            if c % 4 == 0:
                xe = keep.tile([P, 4 * NT], BF16, name="gate%d" % c, align_bytes=256)
                nc.sync.dma_start(out=xe[:], in_=x_edge_c[:, c * NT : (c + 4) * NT])
                gate.extend([xe[:, i * NT : (i + 1) * NT] for i in range(4)])
        split(w2, 1, load_words(W2_words, "w2_catch_up", 0, 2, NT, 2 * NT))
        for g in range(2, G2):
            split(w2, 0, load_words(W2_words, "w2_low_%d" % g, g, g + 1, 0, 2 * NT))
        for g in range(2):
            split(w2, 2, load_words(W2_words, "w2_high_%d" % g, g, g + 1, 2 * NT, 4 * NT))
        for n, g_end in ((2, G2), (3, G2 - 2)):
            for g in range(2, g_end, 2):
                split(w2, n, load_words(W2_words, "w2_%d_%d" % (n, g), g, g + 2, n * NT, (n + 1) * NT))
        n0 = (C2 - 1) * NT
        half = NT // 2
        w2a = {g: w2[3][g][:, 0:half] for g in range(G2 - 2)}
        w2b = {g: w2[3][g][:, half:NT] for g in range(G2 - 2)}
        w2a.update(load_words(W2_words, "w2_a", G2 - 2, G2, n0, n0 + half))
        for g in range(G2 - 2, G2):
            w2b.update(load_words(W2_words, "w2_b%d" % g, g, g + 1, n0 + half, n0 + NT))

        bias1 = []
        bias2 = []

        def spread_matmuls(rows, pair, bank_i):
            ps = bank(bank_i, [P, 2, NT], BF16)
            for i in range(2):
                c = 2 * pair + i
                nc.tensor.matmul(
                    out=ps[:, i, :], lhsT=pick[:, c : c + 1].to_broadcast([P, P]), rhs=rows[:], start=True, stop=True
                )
            return ps

        def copy_bias1(ps, pair):
            t = keep.tile([P, 2, NT], BF16, name="bias1_%d" % pair)
            nc.scalar.copy(
                out=t[:].bitcast(F32).rearrange("p c (u m) -> p c u m", u=2),
                in_=ps[:].bitcast(F32).rearrange("p c (m u) -> p c u m", u=2),
            )
            bias1.extend([t[:, 0, :], t[:, 1, :]])

        def copy_bias2(ps, pair):
            t = keep.tile([P, 2, NT], BF16, name="bias2_%d" % pair)
            nc.scalar.copy(out=t[:], in_=ps[:])
            bias2.extend([t[:, 0, :], t[:, 1, :]])

        xq = {}

        def quantize(src, name, width):
            codes = keep.tile([P, width], U32, name=name + "_codes", align_bytes=64)
            scales = keep.tile([P, width], U8, name=name + "_scales", align_bytes=64)
            nc.vector.quantize_mx(out=codes[:].bitcast(FP8X4), scales=scales[:], in_=src)
            return codes, scales

        ori_wide = []
        for g in range(G1):
            t = keep.tile([P, KP], BF16, name="ori_wide%d" % g)
            codes = ori_u8[:, g * KP : (g + 1) * KP].bitcast(FP8)
            if g < 2:
                nc.vector.tensor_copy(
                    out=t[:].rearrange("p (u m e) -> p m u e", u=2, e=2),
                    in_=codes.rearrange("p (m u e) -> p m u e", u=2, e=2),
                )
            else:
                nc.scalar.copy(
                    out=t[:].rearrange("p (u m e) -> p u m e", u=2, e=2),
                    in_=codes.rearrange("p (m u e) -> p u m e", u=2, e=2),
                )
            ori_wide.append(t)

        for pair in range(2):
            copy_bias1(spread_matmuls(b1_rows, pair, 6 + pair), pair)

        ori_t = []
        for pair in range(2):
            ps = bank(2 + pair, [P, 2, 2, P], F32)
            for i in range(2):
                words = ori_wide[2 * pair + i][:].bitcast(F32)
                for u in range(2):
                    nc.tensor.transpose(ps[:, i, u, :], words[:, P * u : P * (u + 1)], ident[:])
            ori_t.append(ps)
        node_words = node[:].bitcast(F32)
        node_t = []
        for pair in range(2):
            ps = bank(4 + pair, [P, 2, 2, P], F32)
            for i in range(2):
                g = 2 * pair + i
                for u in range(2):
                    nc.tensor.transpose(ps[:, i, u, :], node_words[:, 256 * g + u : 256 * (g + 1) : 2], ident[:])
            node_t.append(ps)

        x_grouped = {}
        for g in range(G1):
            xg = work.tile([P, 4 * P], BF16, name="xg_node", tag="xg_node", bufs=4, align_bytes=64)
            nc.scalar.copy(
                out=xg[:].bitcast(F32).rearrange("p (r u) -> p r u", u=2),
                in_=node_t[g // 2][:, g % 2, :, :].rearrange("p u r -> p r u"),
            )
            x_grouped[g, 0] = xg

        def scale_ori(g):
            xg = work.tile([P, 4 * P], BF16, name="xg_ori", tag="xg_ori", bufs=2, align_bytes=64)
            src = ori_t[g // 2][:, g % 2, :, :].bitcast(BF16).rearrange("p u (r e) -> p r u e", e=2)
            fac = ori_s[:, g, :].rearrange("p (u e) -> p u e", u=2).unsqueeze(1).to_broadcast([P, P, 2, 2])
            nc.vector.tensor_tensor(out=xg[:].rearrange("p (r u e) -> p r u e", u=2, e=2), in0=src, in1=fac, op=MULT)
            x_grouped[g, 1] = xg

        for g0, order in ((0, (1, 0)), (2, (0, 1))):
            scale_ori(g0)
            scale_ori(g0 + 1)
            for j in order:
                for g in (g0, g0 + 1):
                    xq[g, j] = quantize(x_grouped[g, j][:], "xq%d_%d" % (g, j), P)

        for pair in range(2, C1 // 2):
            copy_bias1(spread_matmuls(b1_rows, pair, 4 + pair), pair)

        def mx(acc, stat, j, words, scale_plane, first, last):
            codes, scales = stat
            nc.tensor.matmul_mx(
                out=acc,
                lhsT=codes[:, j * P : (j + 1) * P].bitcast(FP8X4),
                lhsT_scale=scales[:, j * P : (j + 1) * P],
                rhs=words.bitcast(FP8X4),
                rhs_scale=scale_plane,
                start=first,
                stop=last,
            )

        h = {}
        h_t = {}
        h_grouped = {}
        hq = {}

        def stage1_matmuls(c0):
            acc = {(c, j): bank(2 * (c - c0) + j, [P, NT], F32) for c in (c0, c0 + 1) for j in range(2)}
            for g in range(G1):
                for c, j in acc:
                    mx(acc[c, j][:], xq[g, j], 0, w1[c][g], s1[c][4 * g : P, :], g == 0, g == G1 - 1)
            return acc

        def bias_silu(acc, bias, permute):
            width = acc.shape[1]
            pre = work.tile([P, width], F32, name="pre", tag="pre", bufs=4)
            if permute:
                nc.vector.tensor_tensor(
                    out=pre[:].rearrange("p (u m e) -> p u m e", u=2, e=2),
                    in0=acc.rearrange("p (m u e) -> p u m e", u=2, e=2),
                    in1=bias.rearrange("p (u m e) -> p u m e", u=2, e=2),
                    op=ADD,
                )
            else:
                nc.vector.tensor_tensor(out=pre[:], in0=acc, in1=bias, op=ADD)
            act = work.tile([P, width], F32, name="act", tag="act", bufs=4)
            nc.scalar.activation(out=act[:], in_=pre[:], func=SILU)
            return act

        def apply_gate(c, j, act):
            t = work.tile([P, NT], BF16, name="h", tag="h", bufs=4)
            nc.vector.tensor_tensor(
                out=t[:].rearrange("p (u m e) -> p u m e", u=2, e=2),
                in0=act[:].rearrange("p (u m e) -> p u m e", u=2, e=2),
                in1=gate[c].rearrange("p (m u e) -> p u m e", u=2, e=2),
                op=MULT,
            )
            h[c, j] = t

        def transpose_h(c):
            ps = bank(4 + c % 2, [P, 2, 2, P], F32)
            for j in range(2):
                words = h[c, j][:].bitcast(F32)
                for u in range(2):
                    nc.tensor.transpose(ps[:, j, u, :], words[:, P * u : P * (u + 1)], ident[:])
            h_t[c] = ps

        def copy_h(c, on_vector):
            t = work.tile([P, 2 * 4 * P], BF16, name="hg", tag="hg", align_bytes=64)
            dst = t[:].bitcast(F32).rearrange("p (j r u) -> p j r u", j=2, u=2)
            src = h_t[c][:].rearrange("p j u r -> p j r u")
            if on_vector:
                nc.vector.tensor_copy(out=dst, in_=src)
            else:
                nc.scalar.copy(out=dst, in_=src)
            h_grouped[c] = t

        def quantize_h(c):
            hq[c] = quantize(h_grouped[c][:], "hq%d" % c, 2 * P)

        def stage2_pass(acc, g, words, n0, n1):
            for j in range(2):
                mx(acc[j][:], hq[g], j, words, s2[g // 4][4 * (g % 4) : P, n0:n1], g == 0, g == G2 - 1)

        def activate(acc, bias):
            return [bias_silu(acc[j][:], bias, False) for j in range(2)]

        def add_and_store(acts, n0, n1, name):
            res = keep.tile([P, n1 - n0], F32, name=name, align_bytes=256)
            nc.vector.tensor_tensor(out=res[:], in0=acts[0][:], in1=acts[1][:], op=ADD)
            nc.sync.dma_start(out=out2d[:, n0:n1], in_=res[:])

        acc2 = {}

        def stage2_passes(groups, g0, g1):
            for g in range(g0, g1):
                for n in groups:
                    if g == 0:
                        acc2[n] = [bank((6 + 2 * n + j) % 8, [P, NT], F32) for j in range(2)]
                    stage2_pass(acc2[n], g, w2[n][g], n * NT, (n + 1) * NT)

        for c0 in range(0, C1, 2):
            acc = stage1_matmuls(c0)
            if c0 == 0:
                spread = [spread_matmuls(b2_rows, pair, 4 + pair) for pair in range(C2 // 2)]
            else:
                transpose_h(c0 - 2)
                transpose_h(c0 - 1)
            if c0 == 4:
                stage2_passes([0], 0, 2)
            acts = {(c, j): bias_silu(acc[c, j][:], bias1[c], True) for c, j in acc}
            if c0 == 0:
                for pair, ps in enumerate(spread):
                    copy_bias2(ps, pair)
            else:
                copy_h(c0 - 2, False)
                copy_h(c0 - 1, False)
            for c, j in acts:
                apply_gate(c, j, acts[c, j])
            if c0 > 0:
                quantize_h(c0 - 2)
                quantize_h(c0 - 1)

        stage2_passes([1], 0, 2)
        stage2_passes([0, 1], 2, 4)
        transpose_h(6)
        transpose_h(7)
        copy_h(6, False)
        copy_h(7, True)
        quantize_h(6)
        quantize_h(7)
        stage2_passes([0, 1], 4, G2)
        acts_low = [activate(acc2[n], bias2[n]) for n in range(2)]
        for n in range(2):
            add_and_store(acts_low[n], n * NT, (n + 1) * NT, "res%d" % n)
        acc_a = [bank(4 + j, [P, half], F32) for j in range(2)]
        acc_b = [bank(6 + j, [P, half], F32) for j in range(2)]
        for g in range(2):
            stage2_passes([2], g, g + 1)
            stage2_pass(acc_a, g, w2a[g], n0, n0 + half)
            stage2_pass(acc_b, g, w2b[g], n0 + half, n0 + NT)
        stage2_passes([2], 2, G2)
        add_and_store(activate(acc2[2], bias2[2]), 2 * NT, 3 * NT, "res2")
        for g in range(2, G2 - 2):
            stage2_pass(acc_a, g, w2a[g], n0, n0 + half)
            stage2_pass(acc_b, g, w2b[g], n0 + half, n0 + NT)
        for g in range(G2 - 2, G2):
            stage2_pass(acc_a, g, w2a[g], n0, n0 + half)
        acts_a = activate(acc_a, bias2[C2 - 1][:, 0:half])
        for g in range(G2 - 2, G2):
            stage2_pass(acc_b, g, w2b[g], n0 + half, n0 + NT)
        acts_b = activate(acc_b, bias2[C2 - 1][:, half:NT])
        add_and_store(acts_a, n0, n0 + half, "res_a")
        add_and_store(acts_b, n0 + half, n0 + NT, "res_b")
